import numpy as np
import ml_dtypes


def mxq(x, axis, fmt="e4m3"):
    dtype, down = {"e4m3": (ml_dtypes.float8_e4m3fn, 7), "e5m2": (ml_dtypes.float8_e5m2, 14)}[fmt]
    v = np.moveaxis(np.asarray(x, np.float32).astype(ml_dtypes.bfloat16).astype(np.float64), axis, -1)
    blocks = v.reshape(v.shape[:-1] + (-1, 32))
    amax = np.abs(blocks).max(-1, keepdims=True)
    byte = np.maximum(np.where(amax > 0, np.frexp(amax)[1] - 1 + 127, 0) - down, 1)
    scale = np.exp2(byte - 127.0)
    codes = (blocks / scale).astype(np.float32).astype(dtype).astype(np.float64)
    return np.moveaxis((codes * scale).reshape(v.shape), -1, axis)


BF16 = ml_dtypes.bfloat16


def bf(x):
    return np.asarray(x, np.float32).astype(BF16)


def f64(x):
    return np.asarray(x).astype(np.float64)


T, I, O = 4096, 512, 1024


def bit_sign(v):
    return np.where(v > 0, 1.0, -1.0)


def setup_inputs():
    return {"x": bf(np.random.standard_normal((T, I))), "weight": bf(np.random.standard_normal((O, I)) * 0.01)}


def reference(x, weight):
    w_bin = bit_sign(f64(weight))
    div = I ** 0.5
    return (mxq(f64(x), 1, "e4m3") @ mxq(w_bin, 1, "e4m3").T) / div

@@ -1,0 +1,166 @@
+import math
+from contextlib import ExitStack
+
+import concourse.mybir as mybir
+from concourse.masks import make_identity
+
+F32 = mybir.dt.float32
+BF16 = mybir.dt.bfloat16
+U32 = mybir.dt.uint32
+U8 = mybir.dt.uint8
+FP8X4 = mybir.dt.float8_e4m3fn_x4
+ALU = mybir.AluOpType
+ACT = mybir.ActivationFunctionType
+
+P = 128
+T, I, O = 4096, 512, 1024
+FLOPS = 2 * T * I * O
+NT = T // P
+NPAIR = NT // 2
+WORDS = I // 2
+MANUAL = False
+X_CHUNKS = [2,2,4,8,16]
+STORES = [2,2,4,4,4,4,4,4,4]
+AHEAD = 2
+
+
+def tile_blinear_t_kernel(tc, x, weight, out):
+    nc = tc.nc
+    scale = 1.0 / math.sqrt(I)
+    x_rows = x.rearrange("(p j) k -> p (j k)", j=NT)
+    out_rows = out.rearrange("(p j) o -> p (j o)", j=NT)
+    w_rows = weight.rearrange("(r p) k -> p r k", p=P)
+
+    with ExitStack() as ctx:
+        keep = ctx.enter_context(tc.tile_pool(name="keep", bufs=1))
+        stage = ctx.enter_context(tc.tile_pool(name="stage", bufs=4))
+        psum = ctx.enter_context(tc.psum_pool(name="psum", bufs=8))
+        if MANUAL:
+            ctx.enter_context(tc.manual_schedule())
+
+        ident = keep.tile([P, P], F32, name="ident")
+        make_identity(nc, ident[:])
+        warm_in = keep.tile([P, 8], F32, name="warm_in")
+        warm_out = keep.tile([P, 8], F32, name="warm_out")
+        nc.vector.memset(warm_in[:], 0.0)
+        nc.scalar.activation(out=warm_out[:], in_=warm_in[:], func=ACT.Copy, scale=scale)
+
+        w_half = []
+        for h in range(2):
+            wt = keep.tile([P, 4 * I], BF16, name="w%d" % h)
+            nc.sync.dma_start(
+                out=wt[:].rearrange("p (r k) -> p r k", k=I), in_=w_rows[:, 4 * h : 4 * h + 4, :]
+            )
+            w_half.append(wt)
+        x_words = []
+        j0 = 0
+        for c, nj in enumerate(X_CHUNKS):
+            xt = keep.tile([P, nj * I], BF16, name="x%d" % c)
+            nc.sync.dma_start(out=xt[:], in_=x_rows[:, j0 * I : (j0 + nj) * I])
+            xw = xt[:].bitcast(F32)
+            for jj in range(nj):
+                x_words.append(xw[:, jj * WORDS : (jj + 1) * WORDS])
+            j0 += nj
+
+        w_grouped = [keep.tile([P, 4 * 512], BF16, name="wg%d" % h, align_bytes=64) for h in range(2)]
+        w_codes = [keep.tile([P, 512], U32, name="wc%d" % h, align_bytes=64) for h in range(2)]
+        w_scales = [keep.tile([P, 512], U8, name="ws%d" % h, align_bytes=64) for h in range(2)]
+        x_codes = [keep.tile([P, 2 * P], U32, name="xc%d" % g, align_bytes=64) for g in range(NPAIR)]
+        x_scales = [keep.tile([P, 2 * P], U8, name="xs%d" % g, align_bytes=64) for g in range(NPAIR)]
+
+        def transpose_two(words_a, words_b):
+            bank = psum.tile([P, 512], F32, name="bank")
+            for a, words in enumerate((words_a, words_b)):
+                for u in range(2):
+                    q = 2 * a + u
+                    nc.tensor.transpose(bank[:, q * P : (q + 1) * P], words[:, u * P : (u + 1) * P], ident[:])
+            return bank
+
+        def regroup(bank, grouped_bf16):
+            nc.scalar.copy(
+                out=grouped_bf16.bitcast(F32).rearrange("p (a r u) -> p a r u", a=2, u=2),
+                in_=bank[:].rearrange("p (a u r) -> p a r u", a=2, u=2),
+            )
+
+        def sign_a(h, b):
+            v = w_half[h][:, b * 2 * I : (b + 1) * 2 * I]
+            nc.vector.tensor_scalar(out=v, in0=v, scalar1=0.0, scalar2=2.0, op0=ALU.is_gt, op1=ALU.mult)
+
+        def sign_b(h, b):
+            v = w_half[h][:, b * 2 * I : (b + 1) * 2 * I]
+            nc.vector.tensor_scalar(out=v, in0=v, scalar1=-1.0, scalar2=None, op0=ALU.add)
+
+        def w_unit(h, b):
+            ww = w_half[h][:].bitcast(F32)
+            bank = transpose_two(
+                ww[:, (2 * b) * WORDS : (2 * b + 1) * WORDS], ww[:, (2 * b + 1) * WORDS : (2 * b + 2) * WORDS]
+            )
+            regroup(bank, w_grouped[h][:, b * 1024 : (b + 1) * 1024])
+
+        def w_quant(h):
+            nc.vector.quantize_mx(out=w_codes[h][:].bitcast(FP8X4), scales=w_scales[h][:], in_=w_grouped[h][:])
+
+        x_grouped = {}
+
+        def x_unit(g):
+            bank = transpose_two(x_words[2 * g], x_words[2 * g + 1])
+            grouped = stage.tile([P, 1024], BF16, name="grouped", align_bytes=64)
+            regroup(bank, grouped[:])
+            x_grouped[g] = grouped
+
+        def x_quant(g):
+            nc.vector.quantize_mx(
+                out=x_codes[g][:].bitcast(FP8X4), scales=x_scales[g][:], in_=x_grouped[g][:]
+            )
+
+        for h in range(2):
+            sign_a(h, 0)
+            sign_a(h, 1)
+            sign_b(h, 0)
+            sign_b(h, 1)
+            w_unit(h, 0)
+            w_unit(h, 1)
+            x_unit(h)
+            w_quant(h)
+            x_quant(h)
+        for g in range(2, AHEAD):
+            x_unit(g)
+            x_quant(g)
+
+        store_of = []
+        for s, nj in enumerate(STORES):
+            for jj in range(nj):
+                store_of.append((s, jj))
+        out_tiles = [keep.tile([P, nj * O], F32, name="o%d" % s) for s, nj in enumerate(STORES)]
+        first_j = [sum(STORES[:s]) for s in range(len(STORES))]
+
+        for g in range(NPAIR):
+            if g + AHEAD < NPAIR:
+                x_unit(g + AHEAD)
+            n = 0
+            for h in range(2):
+                for a in range(2):
+                    acc = psum.tile([P, 512], F32, name="bank")
+                    nc.tensor.matmul_mx(
+                        out=acc[:],
+                        lhsT=x_codes[g][:, a * P : (a + 1) * P].bitcast(FP8X4),
+                        lhsT_scale=x_scales[g][:, a * P : (a + 1) * P],
+                        rhs=w_codes[h][:].bitcast(FP8X4),
+                        rhs_scale=w_scales[h][:],
+                        start=True,
+                        stop=True,
+                    )
+                    s, jj = store_of[2 * g + a]
+                    dst = out_tiles[s][:, jj * O + h * 512 : jj * O + (h + 1) * 512]
+                    if n % 2 == 0:
+                        nc.scalar.activation(out=dst, in_=acc[:], func=ACT.Copy, scale=scale)
+                    else:
+                        nc.vector.tensor_scalar(out=dst, in0=acc[:], scalar1=scale, scalar2=None, op0=ALU.mult)
+                    n += 1
+            if g + AHEAD < NPAIR:
+                x_quant(g + AHEAD)
+            s, jj = store_of[2 * g + 1]
+            if jj == STORES[s] - 1:
+                nc.sync.dma_start(
+                    out=out_rows[:, first_j[s] * O : (first_j[s] + STORES[s]) * O], in_=out_tiles[s][:]
+                )

@@ -18,18 +18,18 @@ FLOPS = 2 * T * I * O
 NT = T // P
 NPAIR = NT // 2
 WORDS = I // 2
-MANUAL = False
+MANUAL = True
 X_CHUNKS = [2,2,4,8,16]
-STORES = [2,2,4,4,4,4,4,4,4]
-AHEAD = 2
+SPANS = [[0,2],[2,2],[4,2],[6,2],[8,2],[10,2],[12,4],[16,4],[20,4],[24,4],[28,4]]
+PLAN = [("A", 0), ("B", 0), ("A", 1), ("WU", 0, "S"), ("B", 1), ("A", 2), ("WU", 1, "S"), ("A", 3), ("XU", 0, "S"), ("B", 2), ("B", 3), ("QW", 0), ("QX", 0), ("WU", 2, "S"), ("WU", 3, "V"), ("QW", 1), ("MM", 0, 0, "VS"), ("XU", 1, "S"), ("MM", 0, 1, "VS"), ("ST", 0, 2, None), ("QX", 1), ("XU", 2, "V"), ("QX", 2), ("XU", 3, "S"), ("MM", 1, 0, "SV"), ("MM", 1, 1, "SV"), ("ST", 2, 2, None), ("QX", 3), ("XU", 4, "S"), ("MM", 2, 0, "SV"), ("MM", 2, 1, "SV"), ("ST", 4, 2, None), ("QX", 4), ("XU", 5, "S"), ("MM", 3, 0, "SV"), ("MM", 3, 1, "SV"), ("ST", 6, 2, None), ("QX", 5), ("XU", 6, "S"), ("MM", 4, 0, "SV"), ("MM", 4, 1, "SV"), ("ST", 8, 2, None), ("QX", 6), ("XU", 7, "S"), ("MM", 5, 0, "SV"), ("MM", 5, 1, "SV"), ("ST", 10, 2, None), ("QX", 7), ("XU", 8, "S"), ("MM", 6, 0, "SV"), ("MM", 6, 1, "SV"), ("QX", 8), ("XU", 9, "S"), ("MM", 7, 0, "SV"), ("MM", 7, 1, "SV"), ("ST", 12, 4, None), ("QX", 9), ("XU", 10, "S"), ("MM", 8, 0, "SV"), ("MM", 8, 1, "SV"), ("QX", 10), ("XU", 11, "S"), ("MM", 9, 0, "SV"), ("MM", 9, 1, "SV"), ("ST", 16, 4, None), ("QX", 11), ("XU", 12, "S"), ("MM", 10, 0, "SV"), ("MM", 10, 1, "SV"), ("QX", 12), ("XU", 13, "S"), ("MM", 11, 0, "SV"), ("MM", 11, 1, "SV"), ("ST", 20, 4, None), ("QX", 13), ("XU", 14, "S"), ("MM", 12, 0, "SV"), ("MM", 12, 1, "SV"), ("QX", 14), ("XU", 15, "S"), ("MM", 13, 0, "SV"), ("MM", 13, 1, "SV"), ("ST", 24, 4, None), ("QX", 15), ("MM", 14, 0, "SV"), ("MM", 14, 1, "SV"), ("MM", 15, 0, "SV"), ("MM", 15, 1, "SV"), ("ST", 28, 4, None)]
 
 
 def tile_blinear_t_kernel(tc, x, weight, out):
     nc = tc.nc
     scale = 1.0 / math.sqrt(I)
     x_rows = x.rearrange("(p j) k -> p (j k)", j=NT)
-    out_rows = out.rearrange("(p j) o -> p (j o)", j=NT)
-    w_rows = weight.rearrange("(r p) k -> p r k", p=P)
+    out_rows = out.rearrange("(p j) o -> p j o", j=NT)
+    w_rows = weight.rearrange("(q p a) k -> q p (a k)", q=4, a=2)
 
     with ExitStack() as ctx:
         keep = ctx.enter_context(tc.tile_pool(name="keep", bufs=1))
@@ -45,13 +45,11 @@ def tile_blinear_t_kernel(tc, x, weight, out):
         nc.vector.memset(warm_in[:], 0.0)
         nc.scalar.activation(out=warm_out[:], in_=warm_in[:], func=ACT.Copy, scale=scale)
 
-        w_half = []
-        for h in range(2):
-            wt = keep.tile([P, 4 * I], BF16, name="w%d" % h)
-            nc.sync.dma_start(
-                out=wt[:].rearrange("p (r k) -> p r k", k=I), in_=w_rows[:, 4 * h : 4 * h + 4, :]
-            )
-            w_half.append(wt)
+        w_unit_t = []
+        for q in range(4):
+            wt = keep.tile([P, 2 * I], BF16, name="w%d" % q)
+            nc.sync.dma_start(out=wt[:], in_=w_rows[q])
+            w_unit_t.append(wt)
         x_words = []
         j0 = 0
         for c, nj in enumerate(X_CHUNKS):
@@ -67,6 +65,12 @@ def tile_blinear_t_kernel(tc, x, weight, out):
         w_scales = [keep.tile([P, 512], U8, name="ws%d" % h, align_bytes=64) for h in range(2)]
         x_codes = [keep.tile([P, 2 * P], U32, name="xc%d" % g, align_bytes=64) for g in range(NPAIR)]
         x_scales = [keep.tile([P, 2 * P], U8, name="xs%d" % g, align_bytes=64) for g in range(NPAIR)]
+        out_sb = [keep.tile([P, nj, O], F32, name="o%d" % s) for s, (ja, nj) in enumerate(SPANS)]
+        span_of = {}
+        for s, (ja, nj) in enumerate(SPANS):
+            for jj in range(nj):
+                span_of[ja + jj] = (s, jj)
+        x_grouped = {}
 
         def transpose_two(words_a, words_b):
             bank = psum.tile([P, 512], F32, name="bank")
@@ -76,69 +80,48 @@ def tile_blinear_t_kernel(tc, x, weight, out):
                     nc.tensor.transpose(bank[:, q * P : (q + 1) * P], words[:, u * P : (u + 1) * P], ident[:])
             return bank
 
-        def regroup(bank, grouped_bf16):
-            nc.scalar.copy(
-                out=grouped_bf16.bitcast(F32).rearrange("p (a r u) -> p a r u", a=2, u=2),
-                in_=bank[:].rearrange("p (a u r) -> p a r u", a=2, u=2),
-            )
+        def copy_on(eng, dst, src):
+            if eng == "S":
+                nc.scalar.copy(out=dst, in_=src)
+            else:
+                nc.vector.tensor_copy(out=dst, in_=src)
 
-        def sign_a(h, b):
-            v = w_half[h][:, b * 2 * I : (b + 1) * 2 * I]
-            nc.vector.tensor_scalar(out=v, in0=v, scalar1=0.0, scalar2=2.0, op0=ALU.is_gt, op1=ALU.mult)
-
-        def sign_b(h, b):
-            v = w_half[h][:, b * 2 * I : (b + 1) * 2 * I]
-            nc.vector.tensor_scalar(out=v, in0=v, scalar1=-1.0, scalar2=None, op0=ALU.add)
-
-        def w_unit(h, b):
-            ww = w_half[h][:].bitcast(F32)
-            bank = transpose_two(
-                ww[:, (2 * b) * WORDS : (2 * b + 1) * WORDS], ww[:, (2 * b + 1) * WORDS : (2 * b + 2) * WORDS]
-            )
-            regroup(bank, w_grouped[h][:, b * 1024 : (b + 1) * 1024])
-
-        def w_quant(h):
-            nc.vector.quantize_mx(out=w_codes[h][:].bitcast(FP8X4), scales=w_scales[h][:], in_=w_grouped[h][:])
-
-        x_grouped = {}
-
-        def x_unit(g):
-            bank = transpose_two(x_words[2 * g], x_words[2 * g + 1])
-            grouped = stage.tile([P, 1024], BF16, name="grouped", align_bytes=64)
-            regroup(bank, grouped[:])
-            x_grouped[g] = grouped
-
-        def x_quant(g):
-            nc.vector.quantize_mx(
-                out=x_codes[g][:].bitcast(FP8X4), scales=x_scales[g][:], in_=x_grouped[g][:]
-            )
-
-        for h in range(2):
-            sign_a(h, 0)
-            sign_a(h, 1)
-            sign_b(h, 0)
-            sign_b(h, 1)
-            w_unit(h, 0)
-            w_unit(h, 1)
-            x_unit(h)
-            w_quant(h)
-            x_quant(h)
-        for g in range(2, AHEAD):
-            x_unit(g)
-            x_quant(g)
-
-        store_of = []
-        for s, nj in enumerate(STORES):
-            for jj in range(nj):
-                store_of.append((s, jj))
-        out_tiles = [keep.tile([P, nj * O], F32, name="o%d" % s) for s, nj in enumerate(STORES)]
-        first_j = [sum(STORES[:s]) for s in range(len(STORES))]
-
-        for g in range(NPAIR):
-            if g + AHEAD < NPAIR:
-                x_unit(g + AHEAD)
-            n = 0
-            for h in range(2):
+        for step in PLAN:
+            kind = step[0]
+            if kind == "A":
+                v = w_unit_t[step[1]][:]
+                nc.vector.tensor_scalar(out=v, in0=v, scalar1=0.0, scalar2=2.0, op0=ALU.is_gt, op1=ALU.mult)
+            elif kind == "B":
+                v = w_unit_t[step[1]][:]
+                nc.vector.tensor_scalar(out=v, in0=v, scalar1=-1.0, scalar2=None, op0=ALU.add)
+            elif kind == "WU":
+                q = step[1]
+                ww = w_unit_t[q][:].bitcast(F32)
+                bank = transpose_two(ww[:, 0:WORDS], ww[:, WORDS : 2 * WORDS])
+                dst = w_grouped[q // 2][:, (q % 2) * 1024 : (q % 2 + 1) * 1024].bitcast(F32)
+                copy_on(step[2], dst.rearrange("p (r t) -> p r t", t=4), bank[:].rearrange("p (t r) -> p r t", t=4))
+            elif kind == "XU":
+                g = step[1]
+                bank = transpose_two(x_words[2 * g], x_words[2 * g + 1])
+                grouped = stage.tile([P, 1024], BF16, name="grouped", align_bytes=64)
+                copy_on(
+                    step[2],
+                    grouped[:].bitcast(F32).rearrange("p (a r u) -> p a r u", a=2, u=2),
+                    bank[:].rearrange("p (a u r) -> p a r u", a=2, u=2),
+                )
+                x_grouped[g] = grouped
+            elif kind == "QW":
+                h = step[1]
+                nc.vector.quantize_mx(
+                    out=w_codes[h][:].bitcast(FP8X4), scales=w_scales[h][:], in_=w_grouped[h][:]
+                )
+            elif kind == "QX":
+                g = step[1]
+                nc.vector.quantize_mx(
+                    out=x_codes[g][:].bitcast(FP8X4), scales=x_scales[g][:], in_=x_grouped[g][:]
+                )
+            elif kind == "MM":
+                g, h, engs = step[1], step[2], step[3]
                 for a in range(2):
                     acc = psum.tile([P, 512], F32, name="bank")
                     nc.tensor.matmul_mx(
@@ -150,17 +133,17 @@ def tile_blinear_t_kernel(tc, x, weight, out):
                         start=True,
                         stop=True,
                     )
-                    s, jj = store_of[2 * g + a]
-                    dst = out_tiles[s][:, jj * O + h * 512 : jj * O + (h + 1) * 512]
-                    if n % 2 == 0:
+                    s, jj = span_of[2 * g + a]
+                    dst = out_sb[s][:, jj, h * 512 : (h + 1) * 512]
+                    if engs[a] == "S":
                         nc.scalar.activation(out=dst, in_=acc[:], func=ACT.Copy, scale=scale)
                     else:
                         nc.vector.tensor_scalar(out=dst, in0=acc[:], scalar1=scale, scalar2=None, op0=ALU.mult)
-                    n += 1
-            if g + AHEAD < NPAIR:
-                x_quant(g + AHEAD)
-            s, jj = store_of[2 * g + 1]
-            if jj == STORES[s] - 1:
-                nc.sync.dma_start(
-                    out=out_rows[:, first_j[s] * O : (first_j[s] + STORES[s]) * O], in_=out_tiles[s][:]
-                )
+            elif kind == "ST":
+                ja, nj, half = step[1], step[2], step[3]
+                s, jj = span_of[ja]
+                if half is None:
+                    nc.sync.dma_start(out=out_rows[:, ja : ja + nj, :], in_=out_sb[s][:])
+                else:
+                    cols = slice(half * 512, (half + 1) * 512)
+                    nc.sync.dma_start(out=out_rows[:, ja : ja + nj, cols], in_=out_sb[s][:, :, cols])

@@ -18,18 +18,18 @@ FLOPS = 2 * T * I * O
 NT = T // P
 NPAIR = NT // 2
 WORDS = I // 2
-MANUAL = True
-X_CHUNKS = [2,2,4,8,16]
-SPANS = [[0,2],[2,2],[4,2],[6,2],[8,2],[10,2],[12,4],[16,4],[20,4],[24,4],[28,4]]
-PLAN = [("A", 0), ("B", 0), ("A", 1), ("WU", 0, "S"), ("B", 1), ("A", 2), ("WU", 1, "S"), ("A", 3), ("XU", 0, "S"), ("B", 2), ("B", 3), ("QW", 0), ("QX", 0), ("WU", 2, "S"), ("WU", 3, "V"), ("QW", 1), ("MM", 0, 0, "VS"), ("XU", 1, "S"), ("MM", 0, 1, "VS"), ("ST", 0, 2, None), ("QX", 1), ("XU", 2, "V"), ("QX", 2), ("XU", 3, "S"), ("MM", 1, 0, "SV"), ("MM", 1, 1, "SV"), ("ST", 2, 2, None), ("QX", 3), ("XU", 4, "S"), ("MM", 2, 0, "SV"), ("MM", 2, 1, "SV"), ("ST", 4, 2, None), ("QX", 4), ("XU", 5, "S"), ("MM", 3, 0, "SV"), ("MM", 3, 1, "SV"), ("ST", 6, 2, None), ("QX", 5), ("XU", 6, "S"), ("MM", 4, 0, "SV"), ("MM", 4, 1, "SV"), ("ST", 8, 2, None), ("QX", 6), ("XU", 7, "S"), ("MM", 5, 0, "SV"), ("MM", 5, 1, "SV"), ("ST", 10, 2, None), ("QX", 7), ("XU", 8, "S"), ("MM", 6, 0, "SV"), ("MM", 6, 1, "SV"), ("QX", 8), ("XU", 9, "S"), ("MM", 7, 0, "SV"), ("MM", 7, 1, "SV"), ("ST", 12, 4, None), ("QX", 9), ("XU", 10, "S"), ("MM", 8, 0, "SV"), ("MM", 8, 1, "SV"), ("QX", 10), ("XU", 11, "S"), ("MM", 9, 0, "SV"), ("MM", 9, 1, "SV"), ("ST", 16, 4, None), ("QX", 11), ("XU", 12, "S"), ("MM", 10, 0, "SV"), ("MM", 10, 1, "SV"), ("QX", 12), ("XU", 13, "S"), ("MM", 11, 0, "SV"), ("MM", 11, 1, "SV"), ("ST", 20, 4, None), ("QX", 13), ("XU", 14, "S"), ("MM", 12, 0, "SV"), ("MM", 12, 1, "SV"), ("QX", 14), ("XU", 15, "S"), ("MM", 13, 0, "SV"), ("MM", 13, 1, "SV"), ("ST", 24, 4, None), ("QX", 15), ("MM", 14, 0, "SV"), ("MM", 14, 1, "SV"), ("MM", 15, 0, "SV"), ("MM", 15, 1, "SV"), ("ST", 28, 4, None)]
+MANUAL = False
+X_CHUNKS = [2,6,8,16]
+STORES = [2,2,4,4,4,4,4,8]
+AHEAD = 2
 
 
 def tile_blinear_t_kernel(tc, x, weight, out):
     nc = tc.nc
     scale = 1.0 / math.sqrt(I)
     x_rows = x.rearrange("(p j) k -> p (j k)", j=NT)
-    out_rows = out.rearrange("(p j) o -> p j o", j=NT)
-    w_rows = weight.rearrange("(q p a) k -> q p (a k)", q=4, a=2)
+    out_rows = out.rearrange("(p j) o -> p (j o)", j=NT)
+    w_rows = weight.rearrange("(h p r) k -> h p (r k)", h=2, r=4)
 
     with ExitStack() as ctx:
         keep = ctx.enter_context(tc.tile_pool(name="keep", bufs=1))
@@ -45,11 +45,11 @@ def tile_blinear_t_kernel(tc, x, weight, out):
         nc.vector.memset(warm_in[:], 0.0)
         nc.scalar.activation(out=warm_out[:], in_=warm_in[:], func=ACT.Copy, scale=scale)
 
-        w_unit_t = []
-        for q in range(4):
-            wt = keep.tile([P, 2 * I], BF16, name="w%d" % q)
-            nc.sync.dma_start(out=wt[:], in_=w_rows[q])
-            w_unit_t.append(wt)
+        w_half = []
+        for h in range(2):
+            wt = keep.tile([P, 4 * I], BF16, name="w%d" % h)
+            nc.sync.dma_start(out=wt[:], in_=w_rows[h])
+            w_half.append(wt)
         x_words = []
         j0 = 0
         for c, nj in enumerate(X_CHUNKS):
@@ -65,12 +65,6 @@ def tile_blinear_t_kernel(tc, x, weight, out):
         w_scales = [keep.tile([P, 512], U8, name="ws%d" % h, align_bytes=64) for h in range(2)]
         x_codes = [keep.tile([P, 2 * P], U32, name="xc%d" % g, align_bytes=64) for g in range(NPAIR)]
         x_scales = [keep.tile([P, 2 * P], U8, name="xs%d" % g, align_bytes=64) for g in range(NPAIR)]
-        out_sb = [keep.tile([P, nj, O], F32, name="o%d" % s) for s, (ja, nj) in enumerate(SPANS)]
-        span_of = {}
-        for s, (ja, nj) in enumerate(SPANS):
-            for jj in range(nj):
-                span_of[ja + jj] = (s, jj)
-        x_grouped = {}
 
         def transpose_two(words_a, words_b):
             bank = psum.tile([P, 512], F32, name="bank")
@@ -80,48 +74,72 @@ def tile_blinear_t_kernel(tc, x, weight, out):
                     nc.tensor.transpose(bank[:, q * P : (q + 1) * P], words[:, u * P : (u + 1) * P], ident[:])
             return bank
 
-        def copy_on(eng, dst, src):
-            if eng == "S":
-                nc.scalar.copy(out=dst, in_=src)
-            else:
-                nc.vector.tensor_copy(out=dst, in_=src)
+        def regroup(bank, grouped_bf16):
+            nc.scalar.copy(
+                out=grouped_bf16.bitcast(F32).rearrange("p (a r u) -> p a r u", a=2, u=2),
+                in_=bank[:].rearrange("p (a u r) -> p a r u", a=2, u=2),
+            )
 
-        for step in PLAN:
-            kind = step[0]
-            if kind == "A":
-                v = w_unit_t[step[1]][:]
-                nc.vector.tensor_scalar(out=v, in0=v, scalar1=0.0, scalar2=2.0, op0=ALU.is_gt, op1=ALU.mult)
-            elif kind == "B":
-                v = w_unit_t[step[1]][:]
-                nc.vector.tensor_scalar(out=v, in0=v, scalar1=-1.0, scalar2=None, op0=ALU.add)
-            elif kind == "WU":
-                q = step[1]
-                ww = w_unit_t[q][:].bitcast(F32)
-                bank = transpose_two(ww[:, 0:WORDS], ww[:, WORDS : 2 * WORDS])
-                dst = w_grouped[q // 2][:, (q % 2) * 1024 : (q % 2 + 1) * 1024].bitcast(F32)
-                copy_on(step[2], dst.rearrange("p (r t) -> p r t", t=4), bank[:].rearrange("p (t r) -> p r t", t=4))
-            elif kind == "XU":
-                g = step[1]
-                bank = transpose_two(x_words[2 * g], x_words[2 * g + 1])
-                grouped = stage.tile([P, 1024], BF16, name="grouped", align_bytes=64)
-                copy_on(
-                    step[2],
-                    grouped[:].bitcast(F32).rearrange("p (a r u) -> p a r u", a=2, u=2),
-                    bank[:].rearrange("p (a u r) -> p a r u", a=2, u=2),
-                )
-                x_grouped[g] = grouped
-            elif kind == "QW":
-                h = step[1]
-                nc.vector.quantize_mx(
-                    out=w_codes[h][:].bitcast(FP8X4), scales=w_scales[h][:], in_=w_grouped[h][:]
-                )
-            elif kind == "QX":
-                g = step[1]
-                nc.vector.quantize_mx(
-                    out=x_codes[g][:].bitcast(FP8X4), scales=x_scales[g][:], in_=x_grouped[g][:]
-                )
-            elif kind == "MM":
-                g, h, engs = step[1], step[2], step[3]
+        def sign_a(h, b):
+            v = w_half[h][:, b * 2 * I : (b + 1) * 2 * I]
+            nc.vector.tensor_scalar(out=v, in0=v, scalar1=0.0, scalar2=2.0, op0=ALU.is_gt, op1=ALU.mult)
+
+        def sign_b(h, b):
+            v = w_half[h][:, b * 2 * I : (b + 1) * 2 * I]
+            nc.vector.tensor_scalar(out=v, in0=v, scalar1=-1.0, scalar2=None, op0=ALU.add)
+
+        def w_unit(h, b):
+            ww = w_half[h][:].bitcast(F32)
+            bank = transpose_two(
+                ww[:, (2 * b) * WORDS : (2 * b + 1) * WORDS], ww[:, (2 * b + 1) * WORDS : (2 * b + 2) * WORDS]
+            )
+            nc.scalar.copy(
+                out=w_grouped[h][:].bitcast(F32).rearrange("p (r b t) -> p b r t", b=2, t=4)[:, b],
+                in_=bank[:].rearrange("p (t r) -> p r t", t=4),
+            )
+
+        def w_quant(h):
+            nc.vector.quantize_mx(out=w_codes[h][:].bitcast(FP8X4), scales=w_scales[h][:], in_=w_grouped[h][:])
+
+        x_grouped = {}
+
+        def x_unit(g):
+            bank = transpose_two(x_words[2 * g], x_words[2 * g + 1])
+            grouped = stage.tile([P, 1024], BF16, name="grouped", align_bytes=64)
+            regroup(bank, grouped[:])
+            x_grouped[g] = grouped
+
+        def x_quant(g):
+            nc.vector.quantize_mx(
+                out=x_codes[g][:].bitcast(FP8X4), scales=x_scales[g][:], in_=x_grouped[g][:]
+            )
+
+        for h in range(2):
+            sign_a(h, 0)
+            sign_a(h, 1)
+            sign_b(h, 0)
+            sign_b(h, 1)
+            w_unit(h, 0)
+            w_unit(h, 1)
+            x_unit(h)
+            w_quant(h)
+            x_quant(h)
+        for g in range(2, AHEAD):
+            x_unit(g)
+            x_quant(g)
+
+        store_of = []
+        for s, nj in enumerate(STORES):
+            for jj in range(nj):
+                store_of.append((s, jj))
+        out_tiles = [keep.tile([P, nj * O], F32, name="o%d" % s) for s, nj in enumerate(STORES)]
+        first_j = [sum(STORES[:s]) for s in range(len(STORES))]
+
+        for g in range(NPAIR):
+            if g + AHEAD < NPAIR:
+                x_unit(g + AHEAD)
+            n = 0
+            for h in range(2):
                 for a in range(2):
                     acc = psum.tile([P, 512], F32, name="bank")
                     nc.tensor.matmul_mx(
@@ -133,17 +151,17 @@ def tile_blinear_t_kernel(tc, x, weight, out):
                         start=True,
                         stop=True,
                     )
-                    s, jj = span_of[2 * g + a]
-                    dst = out_sb[s][:, jj, h * 512 : (h + 1) * 512]
-                    if engs[a] == "S":
+                    s, jj = store_of[2 * g + a]
+                    dst = out_tiles[s][:, jj * O + h * 512 : jj * O + (h + 1) * 512]
+                    if n % 2 == 0:
                         nc.scalar.activation(out=dst, in_=acc[:], func=ACT.Copy, scale=scale)
                     else:
                         nc.vector.tensor_scalar(out=dst, in0=acc[:], scalar1=scale, scalar2=None, op0=ALU.mult)
-            elif kind == "ST":
-                ja, nj, half = step[1], step[2], step[3]
-                s, jj = span_of[ja]
-                if half is None:
-                    nc.sync.dma_start(out=out_rows[:, ja : ja + nj, :], in_=out_sb[s][:])
-                else:
-                    cols = slice(half * 512, (half + 1) * 512)
-                    nc.sync.dma_start(out=out_rows[:, ja : ja + nj, cols], in_=out_sb[s][:, :, cols])
+                    n += 1
+            if g + AHEAD < NPAIR:
+                x_quant(g + AHEAD)
+            s, jj = store_of[2 * g + 1]
+            if jj == STORES[s] - 1:
+                nc.sync.dma_start(
+                    out=out_rows[:, first_j[s] * O : (first_j[s] + STORES[s]) * O], in_=out_tiles[s][:]
+                )

@@ -18,9 +18,8 @@ FLOPS = 2 * T * I * O
 NT = T // P
 NPAIR = NT // 2
 WORDS = I // 2
-MANUAL = False
 X_CHUNKS = [2,6,8,16]
-STORES = [2,2,4,4,4,4,4,8]
+STORES = [2, 2, 2, 2, 4, 4, 8, 8]
 AHEAD = 2
 
 
@@ -35,8 +34,6 @@ def tile_blinear_t_kernel(tc, x, weight, out):
         keep = ctx.enter_context(tc.tile_pool(name="keep", bufs=1))
         stage = ctx.enter_context(tc.tile_pool(name="stage", bufs=4))
         psum = ctx.enter_context(tc.psum_pool(name="psum", bufs=8))
-        if MANUAL:
-            ctx.enter_context(tc.manual_schedule())
 
         ident = keep.tile([P, P], F32, name="ident")
         make_identity(nc, ident[:])

@@ -19,7 +19,7 @@ NT = T // P
 NPAIR = NT // 2
 WORDS = I // 2
 X_CHUNKS = [2,6,8,16]
-STORES = [2, 2, 2, 2, 4, 4, 8, 8]
+STORES = [2, 2, 2, 4, 4, 6, 6, 6]
 AHEAD = 2
 
 

import math
from contextlib import ExitStack

import concourse.mybir as mybir
from concourse.masks import make_identity

F32 = mybir.dt.float32
BF16 = mybir.dt.bfloat16
U32 = mybir.dt.uint32
U8 = mybir.dt.uint8
FP8X4 = mybir.dt.float8_e4m3fn_x4
ALU = mybir.AluOpType
ACT = mybir.ActivationFunctionType

P = 128
T, I, O = 4096, 512, 1024
FLOPS = 2 * T * I * O
NT = T // P
NPAIR = NT // 2
WORDS = I // 2
X_CHUNKS = [2,6,8,16]
STORES = [2, 2, 2, 4, 4, 6, 6, 6]
AHEAD = 2


def tile_blinear_t_kernel(tc, x, weight, out):
    nc = tc.nc
    scale = 1.0 / math.sqrt(I)
    x_rows = x.rearrange("(p j) k -> p (j k)", j=NT)
    out_rows = out.rearrange("(p j) o -> p (j o)", j=NT)
    w_rows = weight.rearrange("(h p r) k -> h p (r k)", h=2, r=4)

    with ExitStack() as ctx:
        keep = ctx.enter_context(tc.tile_pool(name="keep", bufs=1))
        stage = ctx.enter_context(tc.tile_pool(name="stage", bufs=4))
        psum = ctx.enter_context(tc.psum_pool(name="psum", bufs=8))

        ident = keep.tile([P, P], F32, name="ident")
        make_identity(nc, ident[:])
        warm_in = keep.tile([P, 8], F32, name="warm_in")
        warm_out = keep.tile([P, 8], F32, name="warm_out")
        nc.vector.memset(warm_in[:], 0.0)
        nc.scalar.activation(out=warm_out[:], in_=warm_in[:], func=ACT.Copy, scale=scale)

        w_half = []
        for h in range(2):
            wt = keep.tile([P, 4 * I], BF16, name="w%d" % h)
            nc.sync.dma_start(out=wt[:], in_=w_rows[h])
            w_half.append(wt)
        x_words = []
        j0 = 0
        for c, nj in enumerate(X_CHUNKS):
            xt = keep.tile([P, nj * I], BF16, name="x%d" % c)
            nc.sync.dma_start(out=xt[:], in_=x_rows[:, j0 * I : (j0 + nj) * I])
            xw = xt[:].bitcast(F32)
            for jj in range(nj):
                x_words.append(xw[:, jj * WORDS : (jj + 1) * WORDS])
            j0 += nj

        w_grouped = [keep.tile([P, 4 * 512], BF16, name="wg%d" % h, align_bytes=64) for h in range(2)]
        w_codes = [keep.tile([P, 512], U32, name="wc%d" % h, align_bytes=64) for h in range(2)]
        w_scales = [keep.tile([P, 512], U8, name="ws%d" % h, align_bytes=64) for h in range(2)]
        x_codes = [keep.tile([P, 2 * P], U32, name="xc%d" % g, align_bytes=64) for g in range(NPAIR)]
        x_scales = [keep.tile([P, 2 * P], U8, name="xs%d" % g, align_bytes=64) for g in range(NPAIR)]

        def transpose_two(words_a, words_b):
            bank = psum.tile([P, 512], F32, name="bank")
            for a, words in enumerate((words_a, words_b)):
                for u in range(2):
                    q = 2 * a + u
                    nc.tensor.transpose(bank[:, q * P : (q + 1) * P], words[:, u * P : (u + 1) * P], ident[:])
            return bank

        def regroup(bank, grouped_bf16):
            nc.scalar.copy(
                out=grouped_bf16.bitcast(F32).rearrange("p (a r u) -> p a r u", a=2, u=2),
                in_=bank[:].rearrange("p (a u r) -> p a r u", a=2, u=2),
            )

        def sign_a(h, b):
            v = w_half[h][:, b * 2 * I : (b + 1) * 2 * I]
            nc.vector.tensor_scalar(out=v, in0=v, scalar1=0.0, scalar2=2.0, op0=ALU.is_gt, op1=ALU.mult)

        def sign_b(h, b):
            v = w_half[h][:, b * 2 * I : (b + 1) * 2 * I]
            nc.vector.tensor_scalar(out=v, in0=v, scalar1=-1.0, scalar2=None, op0=ALU.add)

        def w_unit(h, b):
            ww = w_half[h][:].bitcast(F32)
            bank = transpose_two(
                ww[:, (2 * b) * WORDS : (2 * b + 1) * WORDS], ww[:, (2 * b + 1) * WORDS : (2 * b + 2) * WORDS]
            )
            nc.scalar.copy(
                out=w_grouped[h][:].bitcast(F32).rearrange("p (r b t) -> p b r t", b=2, t=4)[:, b],
                in_=bank[:].rearrange("p (t r) -> p r t", t=4),
            )

        def w_quant(h):
            nc.vector.quantize_mx(out=w_codes[h][:].bitcast(FP8X4), scales=w_scales[h][:], in_=w_grouped[h][:])

        x_grouped = {}

        def x_unit(g):
            bank = transpose_two(x_words[2 * g], x_words[2 * g + 1])
            grouped = stage.tile([P, 1024], BF16, name="grouped", align_bytes=64)
            regroup(bank, grouped[:])
            x_grouped[g] = grouped

        def x_quant(g):
            nc.vector.quantize_mx(
                out=x_codes[g][:].bitcast(FP8X4), scales=x_scales[g][:], in_=x_grouped[g][:]
            )

        for h in range(2):
            sign_a(h, 0)
            sign_a(h, 1)
            sign_b(h, 0)
            sign_b(h, 1)
            w_unit(h, 0)
            w_unit(h, 1)
            x_unit(h)
            w_quant(h)
            x_quant(h)
        for g in range(2, AHEAD):
            x_unit(g)
            x_quant(g)

        store_of = []
        for s, nj in enumerate(STORES):
            for jj in range(nj):
                store_of.append((s, jj))
        out_tiles = [keep.tile([P, nj * O], F32, name="o%d" % s) for s, nj in enumerate(STORES)]
        first_j = [sum(STORES[:s]) for s in range(len(STORES))]

        for g in range(NPAIR):
            if g + AHEAD < NPAIR:
                x_unit(g + AHEAD)
            n = 0
            for h in range(2):
                for a in range(2):
                    acc = psum.tile([P, 512], F32, name="bank")
                    nc.tensor.matmul_mx(
                        out=acc[:],
                        lhsT=x_codes[g][:, a * P : (a + 1) * P].bitcast(FP8X4),
                        lhsT_scale=x_scales[g][:, a * P : (a + 1) * P],
                        rhs=w_codes[h][:].bitcast(FP8X4),
                        rhs_scale=w_scales[h][:],
                        start=True,
                        stop=True,
                    )
                    s, jj = store_of[2 * g + a]
                    dst = out_tiles[s][:, jj * O + h * 512 : jj * O + (h + 1) * 512]
                    if n % 2 == 0:
                        nc.scalar.activation(out=dst, in_=acc[:], func=ACT.Copy, scale=scale)
                    else:
                        nc.vector.tensor_scalar(out=dst, in0=acc[:], scalar1=scale, scalar2=None, op0=ALU.mult)
                    n += 1
            if g + AHEAD < NPAIR:
                x_quant(g + AHEAD)
            s, jj = store_of[2 * g + 1]
            if jj == STORES[s] - 1:
                nc.sync.dma_start(
                    out=out_rows[:, first_j[s] * O : (first_j[s] + STORES[s]) * O], in_=out_tiles[s][:]
                )
